import numpy as np
import ml_dtypes


def mxq(x, axis, fmt="e4m3"):
    dtype, down = {"e4m3": (ml_dtypes.float8_e4m3fn, 7), "e5m2": (ml_dtypes.float8_e5m2, 14)}[fmt]
    v = np.moveaxis(np.asarray(x, np.float32).astype(ml_dtypes.bfloat16).astype(np.float64), axis, -1)
    blocks = v.reshape(v.shape[:-1] + (-1, 32))
    amax = np.abs(blocks).max(-1, keepdims=True)
    byte = np.maximum(np.where(amax > 0, np.frexp(amax)[1] - 1 + 127, 0) - down, 1)
    scale = np.exp2(byte - 127.0)
    codes = (blocks / scale).astype(np.float32).astype(dtype).astype(np.float64)
    return np.moveaxis((codes * scale).reshape(v.shape), -1, axis)


WIDE = False


def mx_kscale(k):
    if not WIDE:
        return np.ones(k)
    levels = np.array([10, -10, 5, -5, 0])
    a = np.random.permutation(np.resize(levels, k // 512 * 4)).reshape(k // 512, 4)
    idx = np.arange(k)
    return np.exp2(a[idx // 512, idx % 128 // 32])


BF16 = ml_dtypes.bfloat16


def bf(x):
    return np.asarray(x, np.float32).astype(BF16)


def f64(x):
    return np.asarray(x).astype(np.float64)


N, DIN, DOUT = 1024, 512, 512
C = 1.0


def sigmoid(v):
    return 1.0 / (1.0 + np.exp(-v))


def lorentz_points(gain, spread):
    t = 1.1 + gain * sigmoid(spread * np.random.standard_normal((N, 1)))
    u = np.random.standard_normal((N, DOUT - 1))
    u = u / np.sqrt(np.sum(u * u, axis=1, keepdims=True))
    return np.concatenate([t, u * np.sqrt(t * t - 1.0)], axis=1)


def setup_inputs():
    s = mx_kscale(N)
    q = lorentz_points(4.0, 0.4)
    q[:, :1] *= -1.0
    k = lorentz_points(4.0, 0.4)
    h = lorentz_points(10.0, 1.0)
    adj = (np.random.random((N, N)) < 0.01) * s[None, :]
    return {"q_neg": bf(q), "k": bf(k), "h": bf(h / s[:, None]), "adj": bf(adj),
            "att_bias": bf(7.0 + 0.2 * np.random.standard_normal(1)),
            "att_scale": bf(2.5 * (1.0 + 0.04 * np.random.standard_normal(1)))}


def reference(q_neg, k, h, adj, att_bias, att_scale):
    cin = f64(q_neg) @ f64(k).T
    att = f64(adj) * sigmoid((2.0 + 2.0 * cin) / f64(att_scale) + f64(att_bias))
    support = mxq(att, 1, "e4m3") @ mxq(f64(h), 0, "e4m3")
    l_inner = -support[:, :1] ** 2 + np.sum(support[:, 1:] ** 2, axis=-1, keepdims=True)
    denom = np.sqrt(np.maximum(np.abs(-l_inner), 1e-6)) / np.sqrt(C)
    return support / denom

@@ -1,0 +1,358 @@
+from contextlib import ExitStack
+
+import concourse.mybir as mybir
+from concourse.masks import make_identity
+
+BF16 = mybir.dt.bfloat16
+F32 = mybir.dt.float32
+U32 = mybir.dt.uint32
+U8 = mybir.dt.uint8
+FP8X4 = mybir.dt.float8_e4m3fn_x4
+ACT = mybir.ActivationFunctionType
+ALU = mybir.AluOpType
+
+P = 128
+FLOPS = 2 * 1024 * 1024 * 512 * 2
+
+
+def tile_hybonetconv_pb_kernel(tc, q_neg, k, h, adj, att_bias, att_scale, out):
+    nc = tc.nc
+    with ExitStack() as ctx:
+        keep = ctx.enter_context(tc.tile_pool(name="keep", bufs=1))
+        work = ctx.enter_context(tc.tile_pool(name="work", bufs=3))
+        ps_c = ctx.enter_context(tc.psum_pool(name="ps_c", bufs=3))
+        ps_t = ctx.enter_context(tc.psum_pool(name="ps_t", bufs=3))
+        ps_s = ctx.enter_context(tc.psum_pool(name="ps_s", bufs=2))
+        ctx.enter_context(tc.manual_schedule())
+
+        q_v = q_neg.rearrange("(c p b) d -> c p (b d)", p=P, b=2)
+        k_v = k.rearrange("(c p b) d -> c p (b d)", p=P, b=2)
+        adj_v = adj.rearrange("(c p b) j -> c p (b j)", p=P, b=2)
+        h_v = h.rearrange("(g u p e) f -> g p u (e f)", g=2, u=2, p=P, e=2)
+        out_v = out.rearrange("(c p b) f -> c p (b f)", p=P, b=2)
+
+        ident = keep.tile([P, P], F32, name="ident")
+        make_identity(nc, ident[:])
+        bias_bf = keep.tile([P, 1], BF16, name="bias_bf")
+        scale_bf = keep.tile([P, 1], BF16, name="scale_bf")
+        nc.scalar.dma_start(out=scale_bf[:], in_=att_scale.partition_broadcast(P))
+        nc.scalar.dma_start(out=bias_bf[:], in_=att_bias.partition_broadcast(P))
+        neghalf = keep.tile([P, 2], F32, name="neghalf")
+        nc.vector.memset(neghalf[:], -0.5)
+        warm_in = keep.tile([P, 1], F32, name="warm_in")
+        warm_out = keep.tile([P, 1], F32, name="warm_out")
+        nc.vector.memset(warm_in[:], 0.0)
+        nc.scalar.activation(out=warm_out[:], in_=warm_in[:], func=ACT.Sigmoid)
+
+        q_sb = [keep.tile([P, 1024], BF16, name="q_sb%d" % c) for c in range(4)]
+        k_sb = [keep.tile([P, 1024], BF16, name="k_sb%d" % c) for c in range(4)]
+        adj_sb = [keep.tile([P, 2048], BF16, name="adj_sb%d" % c) for c in range(4)]
+        h_sb = [keep.tile([P, 2048], BF16, name="h_sb%d" % g) for g in range(2)]
+
+        def load_q(c):
+            nc.sync.dma_start(out=q_sb[c][:], in_=q_v[c])
+
+        def load_k(c):
+            nc.sync.dma_start(out=k_sb[c][:], in_=k_v[c])
+
+        def load_adj(c):
+            nc.sync.dma_start(out=adj_sb[c][:], in_=adj_v[c])
+
+        def load_h(g):
+            nc.sync.dma_start(out=h_sb[g][:].rearrange("p (u x) -> p u x", u=2), in_=h_v[g])
+
+        load_q(0)
+        for c in range(4):
+            load_k(c)
+        load_q(1)
+        load_h(0)
+        load_h(1)
+        load_adj(0)
+        load_adj(1)
+        load_q(2)
+        load_adj(2)
+        load_q(3)
+        load_adj(3)
+
+        arg_mul = keep.tile([P, 1], F32, name="arg_mul")
+        arg_add = keep.tile([P, 1], F32, name="arg_add")
+        rec = keep.tile([P, 1], F32, name="rec")
+        nc.vector.reciprocal(out=rec[:], in_=scale_bf[:])
+        nc.vector.tensor_scalar(out=arg_mul[:], in0=rec[:], scalar1=2.0, scalar2=None, op0=ALU.mult)
+        nc.vector.tensor_tensor(out=arg_add[:], in0=arg_mul[:], in1=bias_bf[:], op=ALU.add)
+
+        qT = [keep.tile([P, 1024], BF16, name="qT%d" % c) for c in range(4)]
+        kT = [keep.tile([P, 1024], BF16, name="kT%d" % c) for c in range(4)]
+        hg = [keep.tile([P, 2048], BF16, name="hg%d" % g, align_bytes=64) for g in range(2)]
+        h_codes = [keep.tile([P, 512], U32, name="h_codes%d" % g, align_bytes=64) for g in range(2)]
+        h_scales = [keep.tile([P, 512], U8, name="h_scales%d" % g, align_bytes=64) for g in range(2)]
+        a_codes = [keep.tile([P, 256], U32, name="a_codes%d" % i, align_bytes=64) for i in range(8)]
+        a_scales = [keep.tile([P, 256], U8, name="a_scales%d" % i, align_bytes=64) for i in range(8)]
+        o_sb = [keep.tile([P, 1024], F32, name="o_sb%d" % c) for c in range(4)]
+
+        tr = {}
+        acc = {}
+        sig = {}
+        att = {}
+        sup = {}
+        stat = {}
+        rs = {}
+
+        def new_tr(key):
+            tr[key] = ps_t.tile([P, 512], F32, name="tr", tag="tr")
+
+        def t_rows(key, src, first, wd, b):
+            if first:
+                new_tr(key)
+            words = src[:].bitcast(F32)
+            nc.tensor.transpose(
+                tr[key][:, (wd * 2 + b) * P:(wd * 2 + b + 1) * P],
+                words[:, b * 256 + wd * P: b * 256 + (wd + 1) * P],
+                ident[:],
+            )
+
+        def t_rows_list(key, src):
+            return [
+                (lambda first=(n == 0), wd=n // 2, b=n % 2: t_rows(key, src, first, wd, b))
+                for n in range(4)
+            ]
+
+        def t_adj(iq, g, first, u, b):
+            key = ("a", iq, g)
+            if first:
+                new_tr(key)
+            words = adj_sb[iq][:].bitcast(F32)
+            gu = 2 * g + u
+            nc.tensor.transpose(
+                tr[key][:, (u * 2 + b) * P:(u * 2 + b + 1) * P],
+                words[:, b * 512 + gu * P: b * 512 + (gu + 1) * P],
+                ident[:],
+            )
+
+        def t_adj_list(iq, g):
+            return [
+                (lambda first=(n == 0), u=n // 2, b=n % 2: t_adj(iq, g, first, u, b))
+                for n in range(4)
+            ]
+
+        def copy_out(engine, key, dst):
+            if engine == "v":
+                nc.vector.tensor_copy(out=dst[:].bitcast(F32), in_=tr[key][:])
+            else:
+                nc.scalar.copy(out=dst[:].bitcast(F32), in_=tr[key][:])
+
+        def step(s, extra):
+            iq, gu = divmod(s, 4)
+            acc[s] = ps_c.tile([P, 512], F32, name="acc", tag="acc")
+            kv = kT[gu][:].rearrange("p (w c e) -> p w c e", w=2, e=2)
+            qv = qT[iq][:].rearrange("p (w c e) -> p w c e", w=2, e=2)
+            stride = 1 if len(extra) > 4 else 2
+            n = 0
+            for e in range(2):
+                for wd in range(2):
+                    for ed in range(2):
+                        nc.tensor.matmul(
+                            out=acc[s][:, e * 256:(e + 1) * 256],
+                            lhsT=kv[:, wd, e * P:(e + 1) * P, ed],
+                            rhs=qv[:, wd, :, ed],
+                            start=(wd == 0 and ed == 0),
+                            stop=(wd == 1 and ed == 1),
+                        )
+                        if n % stride == 0 and n // stride < len(extra):
+                            extra[n // stride]()
+                        n += 1
+
+        def sigmoid(s):
+            iq, gu = divmod(s, 4)
+            g, u = divmod(gu, 2)
+            if u == 0:
+                sig[(iq, g)] = work.tile([P, 1024], F32, name="sig", tag="sig", bufs=4)
+            nc.scalar.activation(
+                out=sig[(iq, g)][:, u * 512:(u + 1) * 512].rearrange("p (c e) -> p c e", e=2),
+                in_=acc[s][:].rearrange("p (e c) -> p c e", e=2),
+                func=ACT.Sigmoid,
+                bias=arg_add[:],
+                scale=arg_mul[:],
+            )
+
+        def mult(iq, g):
+            att[(iq, g)] = work.tile([P, 1024], BF16, name="att", tag="att", align_bytes=64)
+            nc.vector.tensor_tensor(
+                out=att[(iq, g)][:].rearrange("p (c u e) -> p c u e", u=2, e=2),
+                in0=sig[(iq, g)][:].rearrange("p (u c e) -> p c u e", u=2, e=2),
+                in1=tr[("a", iq, g)][:].bitcast(BF16).rearrange("p (u c e) -> p c u e", u=2, e=2),
+                op=ALU.mult,
+            )
+
+        def quant(iq, g):
+            nc.vector.quantize_mx(
+                out=a_codes[2 * iq + g][:].bitcast(FP8X4),
+                scales=a_scales[2 * iq + g][:],
+                in_=att[(iq, g)][:],
+            )
+
+        def regroup_h(g):
+            nc.vector.tensor_copy(
+                out=hg[g][:].rearrange("p (c i t) -> p c t i", i=4, t=4),
+                in_=h_sb[g][:].rearrange("p (t c i) -> p c t i", t=4, i=4),
+            )
+
+        def quant_h(g):
+            nc.vector.quantize_mx(
+                out=h_codes[g][:].bitcast(FP8X4), scales=h_scales[g][:], in_=hg[g][:]
+            )
+
+        def mx_pass(iq, b, g):
+            nc.tensor.matmul_mx(
+                out=sup[(iq, b)][:],
+                lhsT=a_codes[2 * iq + g][:, b * P:(b + 1) * P].bitcast(FP8X4),
+                lhsT_scale=a_scales[2 * iq + g][:, b * P:(b + 1) * P],
+                rhs=h_codes[g][:].bitcast(FP8X4),
+                rhs_scale=h_scales[g][:],
+                start=(g == 0),
+                stop=(g == 1),
+            )
+
+        def squares(iq, b):
+            if b == 0:
+                stat[iq] = work.tile([P, 4], F32, name="stat", tag="stat")
+            junk = work.tile([P, 512], BF16, name="junk", tag="junk", bufs=2)
+            nc.scalar.activation(
+                out=junk[:, 0:511], in_=sup[(iq, b)][:, 1:512], func=ACT.Square,
+                accum_out=stat[iq][:, b:b + 1],
+            )
+            nc.scalar.activation(
+                out=stat[iq][:, 2 + b:3 + b], in_=sup[(iq, b)][:, 0:1], func=ACT.Square
+            )
+
+        def chain(iq):
+            nl = work.tile([P, 2], F32, name="nl", tag="nl")
+            al = work.tile([P, 2], F32, name="al", tag="al")
+            cl = work.tile([P, 2], F32, name="cl", tag="cl")
+            rs[iq] = work.tile([P, 2], F32, name="rs", tag="rs")
+            nc.vector.tensor_tensor(out=nl[:], in0=stat[iq][:, 0:2], in1=stat[iq][:, 2:4], op=ALU.subtract)
+            nc.vector.scalar_tensor_tensor(
+                out=al[:], in0=nl[:], scalar=-1.0, in1=nl[:], op0=ALU.mult, op1=ALU.max
+            )
+            nc.vector.tensor_scalar(out=cl[:], in0=al[:], scalar1=1e-6, scalar2=None, op0=ALU.max)
+            nc.gpsimd.tensor_tensor(out=rs[iq][:], in0=cl[:], in1=neghalf[:], op=ALU.pow)
+
+        def scale_v(iq):
+            nc.vector.tensor_scalar(
+                out=o_sb[iq][:, 0:512], in0=sup[(iq, 0)][:], scalar1=rs[iq][:, 0:1], scalar2=None,
+                op0=ALU.mult,
+            )
+
+        def scale_s(iq):
+            nc.scalar.activation(
+                out=o_sb[iq][:, 512:1024], in_=sup[(iq, 1)][:], func=ACT.Copy, scale=rs[iq][:, 1:2]
+            )
+
+        def store(iq):
+            nc.sync.dma_start(out=out_v[iq], in_=o_sb[iq][:])
+
+        def mx_all(iq):
+            for b in range(2):
+                sup[(iq, b)] = ps_s.tile([P, 512], F32, name="sup", tag="sup")
+                for g in range(2):
+                    mx_pass(iq, b, g)
+
+        for f in t_rows_list("q0", q_sb[0]):
+            f()
+        copy_out("v", "q0", qT[0])
+        for f in t_rows_list("k0", k_sb[0]):
+            f()
+        copy_out("s", "k0", kT[0])
+        for f in t_rows_list("k1", k_sb[1]):
+            f()
+        copy_out("v", "k1", kT[1])
+
+        step(0, t_rows_list("k2", k_sb[2]))
+        copy_out("v", "k2", kT[2])
+        sigmoid(0)
+        step(1, t_rows_list("k3", k_sb[3]))
+        copy_out("v", "k3", kT[3])
+        sigmoid(1)
+        step(2, t_rows_list("q1", q_sb[1]))
+        copy_out("v", "q1", qT[1])
+        sigmoid(2)
+        regroup_h(0)
+        regroup_h(1)
+        quant_h(0)
+        quant_h(1)
+        step(3, [])
+        sigmoid(3)
+        step(4, t_adj_list(0, 0))
+        sigmoid(4)
+        mult(0, 0)
+        step(5, t_adj_list(0, 1))
+        sigmoid(5)
+        mult(0, 1)
+        quant(0, 0)
+        step(6, t_rows_list("q2", q_sb[2]) + t_adj_list(1, 0))
+        copy_out("v", "q2", qT[2])
+        quant(0, 1)
+        sigmoid(6)
+        mult(1, 0)
+        step(7, t_adj_list(1, 1))
+        sigmoid(7)
+        quant(1, 0)
+        mult(1, 1)
+        mx_all(0)
+        squares(0, 0)
+        squares(0, 1)
+        quant(1, 1)
+        step(8, t_adj_list(2, 0))
+        sigmoid(8)
+        chain(0)
+        scale_v(0)
+        scale_s(0)
+        store(0)
+        step(9, t_rows_list("q3", q_sb[3]))
+        sigmoid(9)
+        mult(2, 0)
+        copy_out("v", "q3", qT[3])
+        quant(2, 0)
+        step(10, t_adj_list(2, 1))
+        sigmoid(10)
+        mx_all(1)
+        squares(1, 0)
+        squares(1, 1)
+        chain(1)
+        step(11, [])
+        sigmoid(11)
+        scale_s(1)
+        mult(2, 1)
+        scale_v(1)
+        quant(2, 1)
+        store(1)
+        step(12, t_adj_list(3, 0))
+        sigmoid(12)
+        step(13, [])
+        sigmoid(13)
+        mult(3, 0)
+        step(14, t_adj_list(3, 1))
+        sigmoid(14)
+        quant(3, 0)
+        mx_all(2)
+        squares(2, 0)
+        squares(2, 1)
+        chain(2)
+        step(15, [])
+        sigmoid(15)
+        scale_s(2)
+        mult(3, 1)
+        quant(3, 1)
+        scale_v(2)
+        store(2)
+        for b in range(2):
+            sup[(3, b)] = ps_t.tile([P, 512], F32, name="tr", tag="tr")
+            mx_pass(3, b, 0)
+        for b in range(2):
+            mx_pass(3, b, 1)
+        squares(3, 0)
+        squares(3, 1)
+        chain(3)
+        scale_v(3)
+        scale_s(3)
+        store(3)

@@ -30,6 +30,7 @@ def tile_hybonetconv_pb_kernel(tc, q_neg, k, h, adj, att_bias, att_scale, out):
         adj_v = adj.rearrange("(c p b) j -> c p (b j)", p=P, b=2)
         h_v = h.rearrange("(g u p e) f -> g p u (e f)", g=2, u=2, p=P, e=2)
         out_v = out.rearrange("(c p b) f -> c p (b f)", p=P, b=2)
+        out_vb = out.rearrange("(c p b) f -> c b p f", p=P, b=2)
 
         ident = keep.tile([P, P], F32, name="ident")
         make_identity(nc, ident[:])
@@ -86,8 +87,10 @@ def tile_hybonetconv_pb_kernel(tc, q_neg, k, h, adj, att_bias, att_scale, out):
         hg = [keep.tile([P, 2048], BF16, name="hg%d" % g, align_bytes=64) for g in range(2)]
         h_codes = [keep.tile([P, 512], U32, name="h_codes%d" % g, align_bytes=64) for g in range(2)]
         h_scales = [keep.tile([P, 512], U8, name="h_scales%d" % g, align_bytes=64) for g in range(2)]
-        a_codes = [keep.tile([P, 256], U32, name="a_codes%d" % i, align_bytes=64) for i in range(8)]
-        a_scales = [keep.tile([P, 256], U8, name="a_scales%d" % i, align_bytes=64) for i in range(8)]
+        a_codes = [keep.tile([P, 256], U32, name="a_codes%d" % i, align_bytes=64) for i in range(6)]
+        a_scales = [keep.tile([P, 256], U8, name="a_scales%d" % i, align_bytes=64) for i in range(6)]
+        z_codes = [keep.tile([P, P], U32, name="z_codes%d" % i, align_bytes=64) for i in range(4)]
+        z_scales = [keep.tile([P, P], U8, name="z_scales%d" % i, align_bytes=64) for i in range(4)]
         o_sb = [keep.tile([P, 1024], F32, name="o_sb%d" % c) for c in range(4)]
 
         tr = {}
@@ -257,6 +260,116 @@ def tile_hybonetconv_pb_kernel(tc, q_neg, k, h, adj, att_bias, att_scale, out):
                 for g in range(2):
                     mx_pass(iq, b, g)
 
+        def t_adj_one(b, first, g, u):
+            key = ("z", b)
+            if first:
+                new_tr(key)
+            words = adj_sb[3][:].bitcast(F32)
+            gu = 2 * g + u
+            nc.tensor.transpose(
+                tr[key][:, (g * 2 + u) * P:(g * 2 + u + 1) * P],
+                words[:, b * 512 + gu * P: b * 512 + (gu + 1) * P],
+                ident[:],
+            )
+
+        def t_adj_one_list(b):
+            return [
+                (lambda first=(n == 0), g=n // 2, u=n % 2: t_adj_one(b, first, g, u))
+                for n in range(4)
+            ]
+
+        def step_one(b, g):
+            acc[("z", b, g)] = ps_c.tile([P, 512], F32, name="acc", tag="acc")
+            qv = qT[3][:].rearrange("p (w c e) -> p w c e", w=2, e=2)
+            for t in range(4):
+                kv = kT[2 * g + t // 2][:].rearrange("p (w c e) -> p w c e", w=2, e=2)
+                e = t % 2
+                for wd in range(2):
+                    for ed in range(2):
+                        nc.tensor.matmul(
+                            out=acc[("z", b, g)][:, t * P:(t + 1) * P],
+                            lhsT=kv[:, wd, e * P:(e + 1) * P, ed],
+                            rhs=qv[:, wd, b * P:(b + 1) * P, ed],
+                            start=(wd == 0 and ed == 0),
+                            stop=(wd == 1 and ed == 1),
+                        )
+
+        def sigmoid_one(b, g):
+            sig[("z", b, g)] = work.tile([P, 512], F32, name="sigz", tag="sigz")
+            nc.scalar.activation(
+                out=sig[("z", b, g)][:].rearrange("p (c t) -> p c t", t=4),
+                in_=acc[("z", b, g)][:].rearrange("p (t c) -> p c t", t=4),
+                func=ACT.Sigmoid,
+                bias=arg_add[:],
+                scale=arg_mul[:],
+            )
+
+        def mult_one(b, g):
+            att[("z", b, g)] = work.tile([P, 512], BF16, name="attz", tag="attz", align_bytes=64)
+            nc.vector.tensor_tensor(
+                out=att[("z", b, g)][:].rearrange("p (c u e) -> p c u e", u=2, e=2),
+                in0=sig[("z", b, g)][:].rearrange("p (c u e) -> p c u e", u=2, e=2),
+                in1=tr[("z", b)][:, g * 256:(g + 1) * 256].bitcast(BF16).rearrange(
+                    "p (u c e) -> p c u e", u=2, e=2),
+                op=ALU.mult,
+            )
+
+        def quant_one(b, g):
+            nc.vector.quantize_mx(
+                out=z_codes[2 * b + g][:].bitcast(FP8X4),
+                scales=z_scales[2 * b + g][:],
+                in_=att[("z", b, g)][:],
+            )
+
+        def mx_one(b, g):
+            if g == 0:
+                sup[("z", b)] = ps_t.tile([P, 512], F32, name="tr", tag="tr")
+            nc.tensor.matmul_mx(
+                out=sup[("z", b)][:],
+                lhsT=z_codes[2 * b + g][:].bitcast(FP8X4),
+                lhsT_scale=z_scales[2 * b + g][:],
+                rhs=h_codes[g][:].bitcast(FP8X4),
+                rhs_scale=h_scales[g][:],
+                start=(g == 0),
+                stop=(g == 1),
+            )
+
+        def squares_one(b):
+            stat[("z", b)] = work.tile([P, 2], F32, name="statz", tag="statz")
+            junk = work.tile([P, 512], BF16, name="junk", tag="junk", bufs=2)
+            nc.scalar.activation(
+                out=junk[:, 0:511], in_=sup[("z", b)][:, 1:512], func=ACT.Square,
+                accum_out=stat[("z", b)][:, 0:1],
+            )
+            nc.scalar.activation(
+                out=stat[("z", b)][:, 1:2], in_=sup[("z", b)][:, 0:1], func=ACT.Square
+            )
+
+        def chain_one(b):
+            nl = work.tile([P, 1], F32, name="nlz", tag="nlz")
+            al = work.tile([P, 1], F32, name="alz", tag="alz")
+            cl = work.tile([P, 1], F32, name="clz", tag="clz")
+            rs[("z", b)] = work.tile([P, 1], F32, name="rsz", tag="rsz")
+            st = stat[("z", b)]
+            nc.vector.tensor_tensor(out=nl[:], in0=st[:, 0:1], in1=st[:, 1:2], op=ALU.subtract)
+            nc.vector.scalar_tensor_tensor(
+                out=al[:], in0=nl[:], scalar=-1.0, in1=nl[:], op0=ALU.mult, op1=ALU.max
+            )
+            nc.vector.tensor_scalar(out=cl[:], in0=al[:], scalar1=1e-6, scalar2=None, op0=ALU.max)
+            nc.gpsimd.tensor_tensor(out=rs[("z", b)][:], in0=cl[:], in1=neghalf[:, 0:1], op=ALU.pow)
+
+        def scale_one(engine, b):
+            dst = o_sb[3][:, b * 512:(b + 1) * 512]
+            if engine == "v":
+                nc.vector.tensor_scalar(
+                    out=dst, in0=sup[("z", b)][:], scalar1=rs[("z", b)][:], scalar2=None, op0=ALU.mult
+                )
+            else:
+                nc.scalar.activation(out=dst, in_=sup[("z", b)][:], func=ACT.Copy, scale=rs[("z", b)][:])
+
+        def store_one(b):
+            nc.sync.dma_start(out=out_vb[3][b], in_=o_sb[3][:, b * 512:(b + 1) * 512])
+
         for f in t_rows_list("q0", q_sb[0]):
             f()
         copy_out("v", "q0", qT[0])
@@ -319,40 +432,45 @@ def tile_hybonetconv_pb_kernel(tc, q_neg, k, h, adj, att_bias, att_scale, out):
         squares(1, 0)
         squares(1, 1)
         chain(1)
-        step(11, [])
+        step(11, t_adj_one_list(0) + t_adj_one_list(1))
         sigmoid(11)
         scale_s(1)
         mult(2, 1)
         scale_v(1)
         quant(2, 1)
         store(1)
-        step(12, t_adj_list(3, 0))
-        sigmoid(12)
-        step(13, [])
-        sigmoid(13)
-        mult(3, 0)
-        step(14, t_adj_list(3, 1))
-        sigmoid(14)
-        quant(3, 0)
+        step_one(0, 0)
+        sigmoid_one(0, 0)
+        mult_one(0, 0)
+        step_one(0, 1)
+        sigmoid_one(0, 1)
+        quant_one(0, 0)
+        mult_one(0, 1)
+        quant_one(0, 1)
+        step_one(1, 0)
+        sigmoid_one(1, 0)
         mx_all(2)
         squares(2, 0)
         squares(2, 1)
+        mult_one(1, 0)
+        quant_one(1, 0)
         chain(2)
-        step(15, [])
-        sigmoid(15)
+        step_one(1, 1)
+        sigmoid_one(1, 1)
+        mx_one(0, 0)
+        mx_one(0, 1)
+        mx_one(1, 0)
+        mult_one(1, 1)
+        quant_one(1, 1)
+        squares_one(0)
         scale_s(2)
-        mult(3, 1)
-        quant(3, 1)
+        chain_one(0)
         scale_v(2)
         store(2)
-        for b in range(2):
-            sup[(3, b)] = ps_t.tile([P, 512], F32, name="tr", tag="tr")
-            mx_pass(3, b, 0)
-        for b in range(2):
-            mx_pass(3, b, 1)
-        squares(3, 0)
-        squares(3, 1)
-        chain(3)
-        scale_v(3)
-        scale_s(3)
-        store(3)
+        mx_one(1, 1)
+        squares_one(1)
+        scale_one("s", 0)
+        store_one(0)
+        chain_one(1)
+        scale_one("v", 1)
+        store_one(1)

@@ -13,6 +13,10 @@ ALU = mybir.AluOpType
 
 P = 128
 FLOPS = 2 * 1024 * 1024 * 512 * 2
+WARM = 4
+WARM2 = 1
+TAILD = 1
+SPLIT_LAST = True
 
 
 def tile_hybonetconv_pb_kernel(tc, q_neg, k, h, adj, att_bias, att_scale, out):
@@ -27,6 +31,7 @@ def tile_hybonetconv_pb_kernel(tc, q_neg, k, h, adj, att_bias, att_scale, out):
 
         q_v = q_neg.rearrange("(c p b) d -> c p (b d)", p=P, b=2)
         k_v = k.rearrange("(c p b) d -> c p (b d)", p=P, b=2)
+        k_vb = k.rearrange("(c p b) d -> c b p d", p=P, b=2)
         adj_v = adj.rearrange("(c p b) j -> c p (b j)", p=P, b=2)
         h_v = h.rearrange("(g u p e) f -> g p u (e f)", g=2, u=2, p=P, e=2)
         out_v = out.rearrange("(c p b) f -> c p (b f)", p=P, b=2)
@@ -39,6 +44,8 @@ def tile_hybonetconv_pb_kernel(tc, q_neg, k, h, adj, att_bias, att_scale, out):
         nc.scalar.dma_start(out=scale_bf[:], in_=att_scale.partition_broadcast(P))
         nc.scalar.dma_start(out=bias_bf[:], in_=att_bias.partition_broadcast(P))
         neghalf = keep.tile([P, 2], F32, name="neghalf")
+        zeros = keep.tile([P, 256], F32, name="zeros")
+        nc.vector.memset(zeros[:], 0.0)
         nc.vector.memset(neghalf[:], -0.5)
         warm_in = keep.tile([P, 1], F32, name="warm_in")
         warm_out = keep.tile([P, 1], F32, name="warm_out")
@@ -50,30 +57,20 @@ def tile_hybonetconv_pb_kernel(tc, q_neg, k, h, adj, att_bias, att_scale, out):
         adj_sb = [keep.tile([P, 2048], BF16, name="adj_sb%d" % c) for c in range(4)]
         h_sb = [keep.tile([P, 2048], BF16, name="h_sb%d" % g) for g in range(2)]
 
-        def load_q(c):
-            nc.sync.dma_start(out=q_sb[c][:], in_=q_v[c])
+        def load(kind, c):
+            if kind == "q":
+                nc.sync.dma_start(out=q_sb[c][:], in_=q_v[c])
+            elif kind == "k":
+                nc.sync.dma_start(out=k_sb[c][:], in_=k_v[c])
+            elif kind == "k0":
+                nc.sync.dma_start(out=k_sb[0][:, c * 512:(c + 1) * 512], in_=k_vb[0][c])
+            elif kind == "a":
+                nc.sync.dma_start(out=adj_sb[c][:], in_=adj_v[c])
+            else:
+                nc.sync.dma_start(out=h_sb[c][:].rearrange("p (u x) -> p u x", u=2), in_=h_v[c])
 
-        def load_k(c):
-            nc.sync.dma_start(out=k_sb[c][:], in_=k_v[c])
-
-        def load_adj(c):
-            nc.sync.dma_start(out=adj_sb[c][:], in_=adj_v[c])
-
-        def load_h(g):
-            nc.sync.dma_start(out=h_sb[g][:].rearrange("p (u x) -> p u x", u=2), in_=h_v[g])
-
-        load_q(0)
-        for c in range(4):
-            load_k(c)
-        load_q(1)
-        load_h(0)
-        load_h(1)
-        load_adj(0)
-        load_adj(1)
-        load_q(2)
-        load_adj(2)
-        load_q(3)
-        load_adj(3)
+        for kind, c in (("q", 0), ("k0", 0), ("k0", 1), ("k", 1), ("k", 2), ("k", 3), ("q", 1), ("a", 0), ("h", 0), ("h", 1), ("a", 1), ("q", 2), ("a", 2), ("q", 3), ("a", 3)):
+            load(kind, c)
 
         arg_mul = keep.tile([P, 1], F32, name="arg_mul")
         arg_add = keep.tile([P, 1], F32, name="arg_add")
@@ -87,56 +84,72 @@ def tile_hybonetconv_pb_kernel(tc, q_neg, k, h, adj, att_bias, att_scale, out):
         hg = [keep.tile([P, 2048], BF16, name="hg%d" % g, align_bytes=64) for g in range(2)]
         h_codes = [keep.tile([P, 512], U32, name="h_codes%d" % g, align_bytes=64) for g in range(2)]
         h_scales = [keep.tile([P, 512], U8, name="h_scales%d" % g, align_bytes=64) for g in range(2)]
-        a_codes = [keep.tile([P, 256], U32, name="a_codes%d" % i, align_bytes=64) for i in range(6)]
-        a_scales = [keep.tile([P, 256], U8, name="a_scales%d" % i, align_bytes=64) for i in range(6)]
-        z_codes = [keep.tile([P, P], U32, name="z_codes%d" % i, align_bytes=64) for i in range(4)]
-        z_scales = [keep.tile([P, P], U8, name="z_scales%d" % i, align_bytes=64) for i in range(4)]
         o_sb = [keep.tile([P, 1024], F32, name="o_sb%d" % c) for c in range(4)]
 
         tr = {}
         acc = {}
         sig = {}
         att = {}
+        codes = {}
+        planes = {}
+        widths = {}
         sup = {}
         stat = {}
         rs = {}
 
+        def dummy(n, width):
+            for i in range(n):
+                scratch = ps_c.tile([P, width], F32, name="acc", tag="acc")
+                nc.tensor.matmul(out=scratch[:], lhsT=zeros[:, 0:P], rhs=zeros[:, 0:width], start=True, stop=True)
+
         def new_tr(key):
             tr[key] = ps_t.tile([P, 512], F32, name="tr", tag="tr")
 
-        def t_rows(key, src, first, wd, b):
-            if first:
+        def t_rows(key, src, n):
+            wd, b = divmod(n, 2)
+            if n == 0:
                 new_tr(key)
-            words = src[:].bitcast(F32)
             nc.tensor.transpose(
-                tr[key][:, (wd * 2 + b) * P:(wd * 2 + b + 1) * P],
-                words[:, b * 256 + wd * P: b * 256 + (wd + 1) * P],
+                tr[key][:, n * P:(n + 1) * P],
+                src[:].bitcast(F32)[:, b * 256 + wd * P: b * 256 + (wd + 1) * P],
                 ident[:],
             )
 
         def t_rows_list(key, src):
-            return [
-                (lambda first=(n == 0), wd=n // 2, b=n % 2: t_rows(key, src, first, wd, b))
-                for n in range(4)
-            ]
+            return [(lambda n=n: t_rows(key, src, n)) for n in range(4)]
 
-        def t_adj(iq, g, first, u, b):
-            key = ("a", iq, g)
-            if first:
-                new_tr(key)
-            words = adj_sb[iq][:].bitcast(F32)
+        def t_head(key, pool, src, pieces):
+            if pool == "s":
+                tr[key] = ps_s.tile([P, 256], F32, name="sup", tag="sup")
+            else:
+                tr[key] = ps_t.tile([P, 256], F32, name="tr", tag="tr")
+            for n, (b, wd) in enumerate(pieces):
+                nc.tensor.transpose(
+                    tr[key][:, n * P:(n + 1) * P],
+                    src[:].bitcast(F32)[:, b * 256 + wd * P: b * 256 + (wd + 1) * P],
+                    ident[:],
+                )
+
+        def copy_head(engine, key, dst):
+            src = tr[key][:].rearrange("p (a c) -> p a c", a=2)
+            if engine == "v":
+                nc.vector.tensor_copy(out=dst, in_=src)
+            else:
+                nc.scalar.copy(out=dst, in_=src)
+
+        def t_adj(c, g, n):
+            u, b = divmod(n, 2)
+            if n == 0:
+                new_tr(("a", c, g))
             gu = 2 * g + u
             nc.tensor.transpose(
-                tr[key][:, (u * 2 + b) * P:(u * 2 + b + 1) * P],
-                words[:, b * 512 + gu * P: b * 512 + (gu + 1) * P],
+                tr[("a", c, g)][:, n * P:(n + 1) * P],
+                adj_sb[c][:].bitcast(F32)[:, b * 512 + gu * P: b * 512 + (gu + 1) * P],
                 ident[:],
             )
 
-        def t_adj_list(iq, g):
-            return [
-                (lambda first=(n == 0), u=n // 2, b=n % 2: t_adj(iq, g, first, u, b))
-                for n in range(4)
-            ]
+        def t_adj_list(c, g):
+            return [(lambda n=n: t_adj(c, g, n)) for n in range(4)]
 
         def copy_out(engine, key, dst):
             if engine == "v":
@@ -144,20 +157,20 @@ def tile_hybonetconv_pb_kernel(tc, q_neg, k, h, adj, att_bias, att_scale, out):
             else:
                 nc.scalar.copy(out=dst[:].bitcast(F32), in_=tr[key][:])
 
-        def step(s, extra):
-            iq, gu = divmod(s, 4)
-            acc[s] = ps_c.tile([P, 512], F32, name="acc", tag="acc")
+        def fill(c, gu, lo, w, extra, dense=False):
+            key = (c, gu, lo)
+            acc[key] = ps_c.tile([P, 2 * w], F32, name="acc", tag="acc")
             kv = kT[gu][:].rearrange("p (w c e) -> p w c e", w=2, e=2)
-            qv = qT[iq][:].rearrange("p (w c e) -> p w c e", w=2, e=2)
-            stride = 1 if len(extra) > 4 else 2
+            qv = qT[c][:].rearrange("p (w c e) -> p w c e", w=2, e=2)
+            stride = 1 if (len(extra) > 4 or dense) else 2
             n = 0
             for e in range(2):
                 for wd in range(2):
                     for ed in range(2):
                         nc.tensor.matmul(
-                            out=acc[s][:, e * 256:(e + 1) * 256],
+                            out=acc[key][:, e * w:(e + 1) * w],
                             lhsT=kv[:, wd, e * P:(e + 1) * P, ed],
-                            rhs=qv[:, wd, :, ed],
+                            rhs=qv[:, wd, lo:lo + w, ed],
                             start=(wd == 0 and ed == 0),
                             stop=(wd == 1 and ed == 1),
                         )
@@ -165,312 +178,224 @@ def tile_hybonetconv_pb_kernel(tc, q_neg, k, h, adj, att_bias, att_scale, out):
                             extra[n // stride]()
                         n += 1
 
-        def sigmoid(s):
-            iq, gu = divmod(s, 4)
+        def sigmoid(c, gu, lo, w):
             g, u = divmod(gu, 2)
             if u == 0:
-                sig[(iq, g)] = work.tile([P, 1024], F32, name="sig", tag="sig", bufs=4)
+                sig[(c, g, lo)] = work.tile([P, 4 * w], F32, name="sig", tag="sig", bufs=4)
             nc.scalar.activation(
-                out=sig[(iq, g)][:, u * 512:(u + 1) * 512].rearrange("p (c e) -> p c e", e=2),
-                in_=acc[s][:].rearrange("p (e c) -> p c e", e=2),
+                out=sig[(c, g, lo)][:, u * 2 * w:(u + 1) * 2 * w].rearrange("p (c e) -> p c e", e=2),
+                in_=acc[(c, gu, lo)][:].rearrange("p (e c) -> p c e", e=2),
                 func=ACT.Sigmoid,
                 bias=arg_add[:],
                 scale=arg_mul[:],
             )
 
-        def mult(iq, g):
-            att[(iq, g)] = work.tile([P, 1024], BF16, name="att", tag="att", align_bytes=64)
+        def mult(c, g, lo, w):
+            att[(c, g, lo)] = work.tile([P, 4 * w], BF16, name="att", tag="att", align_bytes=64)
             nc.vector.tensor_tensor(
-                out=att[(iq, g)][:].rearrange("p (c u e) -> p c u e", u=2, e=2),
-                in0=sig[(iq, g)][:].rearrange("p (u c e) -> p c u e", u=2, e=2),
-                in1=tr[("a", iq, g)][:].bitcast(BF16).rearrange("p (u c e) -> p c u e", u=2, e=2),
+                out=att[(c, g, lo)][:].rearrange("p (c u e) -> p c u e", u=2, e=2),
+                in0=sig[(c, g, lo)][:].rearrange("p (u c e) -> p c u e", u=2, e=2),
+                in1=tr[("a", c, g)][:].bitcast(BF16).rearrange(
+                    "p (u c e) -> p c u e", u=2, e=2)[:, lo:lo + w, :, :],
                 op=ALU.mult,
             )
 
-        def quant(iq, g):
+        def quant(c, g, lo, w):
+            widths[(c, g, lo)] = w
+            codes[(c, g, lo)] = keep.tile([P, w], U32, name="codes_%d_%d_%d" % (c, g, lo), align_bytes=64)
+            planes[(c, g, lo)] = keep.tile([P, w], U8, name="planes_%d_%d_%d" % (c, g, lo), align_bytes=64)
             nc.vector.quantize_mx(
-                out=a_codes[2 * iq + g][:].bitcast(FP8X4),
-                scales=a_scales[2 * iq + g][:],
-                in_=att[(iq, g)][:],
+                out=codes[(c, g, lo)][:].bitcast(FP8X4), scales=planes[(c, g, lo)][:], in_=att[(c, g, lo)][:]
             )
 
-        def regroup_h(g):
-            nc.vector.tensor_copy(
-                out=hg[g][:].rearrange("p (c i t) -> p c t i", i=4, t=4),
-                in_=h_sb[g][:].rearrange("p (t c i) -> p c t i", t=4, i=4),
-            )
+        def regroup_h(engine, g, lo, w):
+            dst = hg[g][:, 4 * lo:4 * (lo + w)].rearrange("p (c i t) -> p c t i", i=4, t=4)
+            src = h_sb[g][:].rearrange("p (t f) -> p t f", t=4)[:, :, lo:lo + w].rearrange(
+                "p t (c i) -> p c t i", i=4)
+            if engine == "v":
+                nc.vector.tensor_copy(out=dst, in_=src)
+            else:
+                nc.scalar.copy(out=dst, in_=src)
 
         def quant_h(g):
             nc.vector.quantize_mx(
                 out=h_codes[g][:].bitcast(FP8X4), scales=h_scales[g][:], in_=hg[g][:]
             )
 
-        def mx_pass(iq, b, g):
-            nc.tensor.matmul_mx(
-                out=sup[(iq, b)][:],
-                lhsT=a_codes[2 * iq + g][:, b * P:(b + 1) * P].bitcast(FP8X4),
-                lhsT_scale=a_scales[2 * iq + g][:, b * P:(b + 1) * P],
-                rhs=h_codes[g][:].bitcast(FP8X4),
-                rhs_scale=h_scales[g][:],
-                start=(g == 0),
-                stop=(g == 1),
-            )
-
-        def squares(iq, b):
-            if b == 0:
-                stat[iq] = work.tile([P, 4], F32, name="stat", tag="stat")
-            junk = work.tile([P, 512], BF16, name="junk", tag="junk", bufs=2)
-            nc.scalar.activation(
-                out=junk[:, 0:511], in_=sup[(iq, b)][:, 1:512], func=ACT.Square,
-                accum_out=stat[iq][:, b:b + 1],
-            )
-            nc.scalar.activation(
-                out=stat[iq][:, 2 + b:3 + b], in_=sup[(iq, b)][:, 0:1], func=ACT.Square
-            )
-
-        def chain(iq):
-            nl = work.tile([P, 2], F32, name="nl", tag="nl")
-            al = work.tile([P, 2], F32, name="al", tag="al")
-            cl = work.tile([P, 2], F32, name="cl", tag="cl")
-            rs[iq] = work.tile([P, 2], F32, name="rs", tag="rs")
-            nc.vector.tensor_tensor(out=nl[:], in0=stat[iq][:, 0:2], in1=stat[iq][:, 2:4], op=ALU.subtract)
-            nc.vector.scalar_tensor_tensor(
-                out=al[:], in0=nl[:], scalar=-1.0, in1=nl[:], op0=ALU.mult, op1=ALU.max
-            )
-            nc.vector.tensor_scalar(out=cl[:], in0=al[:], scalar1=1e-6, scalar2=None, op0=ALU.max)
-            nc.gpsimd.tensor_tensor(out=rs[iq][:], in0=cl[:], in1=neghalf[:], op=ALU.pow)
-
-        def scale_v(iq):
-            nc.vector.tensor_scalar(
-                out=o_sb[iq][:, 0:512], in0=sup[(iq, 0)][:], scalar1=rs[iq][:, 0:1], scalar2=None,
-                op0=ALU.mult,
-            )
-
-        def scale_s(iq):
-            nc.scalar.activation(
-                out=o_sb[iq][:, 512:1024], in_=sup[(iq, 1)][:], func=ACT.Copy, scale=rs[iq][:, 1:2]
-            )
-
-        def store(iq):
-            nc.sync.dma_start(out=out_v[iq], in_=o_sb[iq][:])
-
-        def mx_all(iq):
-            for b in range(2):
-                sup[(iq, b)] = ps_s.tile([P, 512], F32, name="sup", tag="sup")
-                for g in range(2):
-                    mx_pass(iq, b, g)
-
-        def t_adj_one(b, first, g, u):
-            key = ("z", b)
-            if first:
-                new_tr(key)
-            words = adj_sb[3][:].bitcast(F32)
-            gu = 2 * g + u
-            nc.tensor.transpose(
-                tr[key][:, (g * 2 + u) * P:(g * 2 + u + 1) * P],
-                words[:, b * 512 + gu * P: b * 512 + (gu + 1) * P],
-                ident[:],
-            )
-
-        def t_adj_one_list(b):
-            return [
-                (lambda first=(n == 0), g=n // 2, u=n % 2: t_adj_one(b, first, g, u))
-                for n in range(4)
-            ]
-
-        def step_one(b, g):
-            acc[("z", b, g)] = ps_c.tile([P, 512], F32, name="acc", tag="acc")
-            qv = qT[3][:].rearrange("p (w c e) -> p w c e", w=2, e=2)
-            for t in range(4):
-                kv = kT[2 * g + t // 2][:].rearrange("p (w c e) -> p w c e", w=2, e=2)
-                e = t % 2
-                for wd in range(2):
-                    for ed in range(2):
-                        nc.tensor.matmul(
-                            out=acc[("z", b, g)][:, t * P:(t + 1) * P],
-                            lhsT=kv[:, wd, e * P:(e + 1) * P, ed],
-                            rhs=qv[:, wd, b * P:(b + 1) * P, ed],
-                            start=(wd == 0 and ed == 0),
-                            stop=(wd == 1 and ed == 1),
-                        )
-
-        def sigmoid_one(b, g):
-            sig[("z", b, g)] = work.tile([P, 512], F32, name="sigz", tag="sigz")
-            nc.scalar.activation(
-                out=sig[("z", b, g)][:].rearrange("p (c t) -> p c t", t=4),
-                in_=acc[("z", b, g)][:].rearrange("p (t c) -> p c t", t=4),
-                func=ACT.Sigmoid,
-                bias=arg_add[:],
-                scale=arg_mul[:],
-            )
-
-        def mult_one(b, g):
-            att[("z", b, g)] = work.tile([P, 512], BF16, name="attz", tag="attz", align_bytes=64)
-            nc.vector.tensor_tensor(
-                out=att[("z", b, g)][:].rearrange("p (c u e) -> p c u e", u=2, e=2),
-                in0=sig[("z", b, g)][:].rearrange("p (c u e) -> p c u e", u=2, e=2),
-                in1=tr[("z", b)][:, g * 256:(g + 1) * 256].bitcast(BF16).rearrange(
-                    "p (u c e) -> p c u e", u=2, e=2),
-                op=ALU.mult,
-            )
-
-        def quant_one(b, g):
-            nc.vector.quantize_mx(
-                out=z_codes[2 * b + g][:].bitcast(FP8X4),
-                scales=z_scales[2 * b + g][:],
-                in_=att[("z", b, g)][:],
-            )
-
-        def mx_one(b, g):
+        def mx_pass(c, b, g, pool, flo, fw):
+            key = (c, b, flo)
             if g == 0:
-                sup[("z", b)] = ps_t.tile([P, 512], F32, name="tr", tag="tr")
+                if pool == "s":
+                    sup[key] = ps_s.tile([P, fw], F32, name="sup", tag="sup")
+                elif pool == "t":
+                    sup[key] = ps_t.tile([P, fw], F32, name="tr", tag="tr")
+                else:
+                    sup[key] = ps_c.tile([P, fw], F32, name="acc", tag="acc")
+            if widths.get((c, g, 0), 0) == 256:
+                cd, pl = codes[(c, g, 0)][:, b * P:(b + 1) * P], planes[(c, g, 0)][:, b * P:(b + 1) * P]
+            else:
+                cd, pl = codes[(c, g, b * P)][:], planes[(c, g, b * P)][:]
             nc.tensor.matmul_mx(
-                out=sup[("z", b)][:],
-                lhsT=z_codes[2 * b + g][:].bitcast(FP8X4),
-                lhsT_scale=z_scales[2 * b + g][:],
-                rhs=h_codes[g][:].bitcast(FP8X4),
-                rhs_scale=h_scales[g][:],
+                out=sup[key][:],
+                lhsT=cd.bitcast(FP8X4),
+                lhsT_scale=pl,
+                rhs=h_codes[g][:, flo:flo + fw].bitcast(FP8X4),
+                rhs_scale=h_scales[g][:, flo:flo + fw],
                 start=(g == 0),
                 stop=(g == 1),
             )
 
-        def squares_one(b):
-            stat[("z", b)] = work.tile([P, 2], F32, name="statz", tag="statz")
+        def squares(c, b, first):
+            if first:
+                stat[c] = work.tile([P, 4], F32, name="stat", tag="stat", bufs=4)
             junk = work.tile([P, 512], BF16, name="junk", tag="junk", bufs=2)
             nc.scalar.activation(
-                out=junk[:, 0:511], in_=sup[("z", b)][:, 1:512], func=ACT.Square,
-                accum_out=stat[("z", b)][:, 0:1],
+                out=junk[:, 0:511], in_=sup[(c, b, 0)][:, 1:512], func=ACT.Square,
+                accum_out=stat[c][:, b:b + 1],
             )
             nc.scalar.activation(
-                out=stat[("z", b)][:, 1:2], in_=sup[("z", b)][:, 0:1], func=ACT.Square
+                out=stat[c][:, 2 + b:3 + b], in_=sup[(c, b, 0)][:, 0:1], func=ACT.Square
             )
 
-        def chain_one(b):
-            nl = work.tile([P, 1], F32, name="nlz", tag="nlz")
-            al = work.tile([P, 1], F32, name="alz", tag="alz")
-            cl = work.tile([P, 1], F32, name="clz", tag="clz")
-            rs[("z", b)] = work.tile([P, 1], F32, name="rsz", tag="rsz")
-            st = stat[("z", b)]
-            nc.vector.tensor_tensor(out=nl[:], in0=st[:, 0:1], in1=st[:, 1:2], op=ALU.subtract)
+        def chain(c, b, n):
+            nl = work.tile([P, n], F32, name="nl", tag="nl")
+            al = work.tile([P, n], F32, name="al", tag="al")
+            cl = work.tile([P, n], F32, name="cl", tag="cl")
+            rs[(c, b)] = work.tile([P, n], F32, name="rs", tag="rs", bufs=4)
+            nc.vector.tensor_tensor(
+                out=nl[:], in0=stat[c][:, b:b + n], in1=stat[c][:, 2 + b:2 + b + n], op=ALU.subtract)
             nc.vector.scalar_tensor_tensor(
                 out=al[:], in0=nl[:], scalar=-1.0, in1=nl[:], op0=ALU.mult, op1=ALU.max
             )
             nc.vector.tensor_scalar(out=cl[:], in0=al[:], scalar1=1e-6, scalar2=None, op0=ALU.max)
-            nc.gpsimd.tensor_tensor(out=rs[("z", b)][:], in0=cl[:], in1=neghalf[:, 0:1], op=ALU.pow)
+            nc.gpsimd.tensor_tensor(out=rs[(c, b)][:], in0=cl[:], in1=neghalf[:, 0:n], op=ALU.pow)
 
-        def scale_one(engine, b):
-            dst = o_sb[3][:, b * 512:(b + 1) * 512]
+        def scale(engine, c, b, r, flo=0, fw=512):
+            dst = o_sb[c][:, b * 512 + flo:b * 512 + flo + fw]
             if engine == "v":
-                nc.vector.tensor_scalar(
-                    out=dst, in0=sup[("z", b)][:], scalar1=rs[("z", b)][:], scalar2=None, op0=ALU.mult
-                )
+                nc.vector.tensor_scalar(out=dst, in0=sup[(c, b, flo)][:], scalar1=r, scalar2=None, op0=ALU.mult)
             else:
-                nc.scalar.activation(out=dst, in_=sup[("z", b)][:], func=ACT.Copy, scale=rs[("z", b)][:])
+                nc.scalar.activation(out=dst, in_=sup[(c, b, flo)][:], func=ACT.Copy, scale=r)
 
-        def store_one(b):
-            nc.sync.dma_start(out=out_vb[3][b], in_=o_sb[3][:, b * 512:(b + 1) * 512])
+        def store(c):
+            nc.sync.dma_start(out=out_v[c], in_=o_sb[c][:])
 
-        for f in t_rows_list("q0", q_sb[0]):
-            f()
-        copy_out("v", "q0", qT[0])
-        for f in t_rows_list("k0", k_sb[0]):
-            f()
-        copy_out("s", "k0", kT[0])
+        def store_block(c, b):
+            nc.sync.dma_start(out=out_vb[c][b], in_=o_sb[c][:, b * 512:(b + 1) * 512])
+
+        def mx_all(c):
+            for b in range(2):
+                for g in range(2):
+                    mx_pass(c, b, g, "s", 0, 512)
+
+        dummy(WARM, 256)
+        t_head("q0a", "t", q_sb[0], ((0, 0), (1, 0)))
+        t_head("q0b", "t", q_sb[0], ((0, 1), (1, 1)))
+        copy_head("v", "q0a", qT[0][:].bitcast(F32)[:, 0:256].rearrange("p (a c) -> p a c", a=2))
+        copy_head("s", "q0b", qT[0][:].bitcast(F32)[:, 256:512].rearrange("p (a c) -> p a c", a=2))
+        t_head("k0a", "s", k_sb[0], ((0, 0), (0, 1)))
+        copy_head("v", "k0a", kT[0][:].bitcast(F32).rearrange("p (w e c) -> p w e c", w=2, e=2)[:, :, 0, :])
+        dummy(WARM2, 128)
+        t_head("k0b", "s", k_sb[0], ((1, 0), (1, 1)))
+        copy_head("s", "k0b", kT[0][:].bitcast(F32).rearrange("p (w e c) -> p w e c", w=2, e=2)[:, :, 1, :])
+        dummy(WARM2, 128)
         for f in t_rows_list("k1", k_sb[1]):
             f()
         copy_out("v", "k1", kT[1])
-
-        step(0, t_rows_list("k2", k_sb[2]))
+        fill(0, 0, 0, 256, t_rows_list("k2", k_sb[2]))
         copy_out("v", "k2", kT[2])
-        sigmoid(0)
-        step(1, t_rows_list("k3", k_sb[3]))
+        sigmoid(0, 0, 0, 256)
+        fill(0, 1, 0, 256, t_rows_list("k3", k_sb[3]))
         copy_out("v", "k3", kT[3])
-        sigmoid(1)
-        step(2, t_rows_list("q1", q_sb[1]))
+        sigmoid(0, 1, 0, 256)
+        fill(0, 2, 0, 256, t_rows_list("q1", q_sb[1]) + t_adj_list(0, 0))
         copy_out("v", "q1", qT[1])
-        sigmoid(2)
-        regroup_h(0)
-        regroup_h(1)
-        quant_h(0)
+        sigmoid(0, 2, 0, 256)
+        mult(0, 0, 0, 256)
+        fill(0, 3, 0, 256, t_adj_list(0, 1))
+        sigmoid(0, 3, 0, 256)
+        regroup_h("s", 0, 0, 256)
+        regroup_h("v", 1, 0, 512)
+        quant(0, 0, 0, 256)
+        mult(0, 1, 0, 256)
+        fill(1, 0, 0, 256, [])
+        sigmoid(1, 0, 0, 256)
+        regroup_h("s", 0, 256, 256)
+        quant(0, 1, 0, 256)
         quant_h(1)
-        step(3, [])
-        sigmoid(3)
-        step(4, t_adj_list(0, 0))
-        sigmoid(4)
-        mult(0, 0)
-        step(5, t_adj_list(0, 1))
-        sigmoid(5)
-        mult(0, 1)
-        quant(0, 0)
-        step(6, t_rows_list("q2", q_sb[2]) + t_adj_list(1, 0))
+        fill(1, 1, 0, 256, t_adj_list(1, 0))
+        sigmoid(1, 1, 0, 256)
+        quant_h(0)
+        mult(1, 0, 0, 256)
+        fill(1, 2, 0, 256, t_rows_list("q2", q_sb[2]) + t_adj_list(1, 1))
         copy_out("v", "q2", qT[2])
-        quant(0, 1)
-        sigmoid(6)
-        mult(1, 0)
-        step(7, t_adj_list(1, 1))
-        sigmoid(7)
-        quant(1, 0)
-        mult(1, 1)
+        sigmoid(1, 2, 0, 256)
+        quant(1, 0, 0, 256)
+        fill(1, 3, 0, 256, [])
+        sigmoid(1, 3, 0, 256)
+        mult(1, 1, 0, 256)
         mx_all(0)
-        squares(0, 0)
-        squares(0, 1)
-        quant(1, 1)
-        step(8, t_adj_list(2, 0))
-        sigmoid(8)
-        chain(0)
-        scale_v(0)
-        scale_s(0)
+        squares(0, 0, True)
+        squares(0, 1, False)
+        quant(1, 1, 0, 256)
+        fill(2, 0, 0, 256, t_adj_list(2, 0))
+        sigmoid(2, 0, 0, 256)
+        chain(0, 0, 2)
+        scale("v", 0, 0, rs[(0, 0)][:, 0:1])
+        scale("s", 0, 1, rs[(0, 0)][:, 1:2])
         store(0)
-        step(9, t_rows_list("q3", q_sb[3]))
-        sigmoid(9)
-        mult(2, 0)
+        fill(2, 1, 0, 256, t_rows_list("q3", q_sb[3]))
+        sigmoid(2, 1, 0, 256)
+        mult(2, 0, 0, 256)
         copy_out("v", "q3", qT[3])
-        quant(2, 0)
-        step(10, t_adj_list(2, 1))
-        sigmoid(10)
+        quant(2, 0, 0, 256)
+        fill(2, 2, 0, 256, t_adj_list(2, 1))
+        sigmoid(2, 2, 0, 256)
         mx_all(1)
-        squares(1, 0)
-        squares(1, 1)
-        chain(1)
-        step(11, t_adj_one_list(0) + t_adj_one_list(1))
-        sigmoid(11)
-        scale_s(1)
-        mult(2, 1)
-        scale_v(1)
-        quant(2, 1)
+        squares(1, 0, True)
+        squares(1, 1, False)
+        chain(1, 0, 2)
+        fill(2, 3, 0, 256, t_adj_list(3, 0))
+        sigmoid(2, 3, 0, 256)
+        scale("s", 1, 1, rs[(1, 0)][:, 1:2])
+        mult(2, 1, 0, 256)
+        scale("v", 1, 0, rs[(1, 0)][:, 0:1])
+        quant(2, 1, 0, 256)
         store(1)
-        step_one(0, 0)
-        sigmoid_one(0, 0)
-        mult_one(0, 0)
-        step_one(0, 1)
-        sigmoid_one(0, 1)
-        quant_one(0, 0)
-        mult_one(0, 1)
-        quant_one(0, 1)
-        step_one(1, 0)
-        sigmoid_one(1, 0)
+        fill(3, 0, 0, 256, t_adj_list(3, 1))
+        sigmoid(3, 0, 0, 256)
+        fill(3, 1, 0, 256, [])
+        sigmoid(3, 1, 0, 256)
+        mult(3, 0, 0, 256)
+        quant(3, 0, 0, 256)
+        fill(3, 2, 0, 128, [])
+        sigmoid(3, 2, 0, 128)
+        fill(3, 3, 0, 128, [])
+        sigmoid(3, 3, 0, 128)
         mx_all(2)
-        squares(2, 0)
-        squares(2, 1)
-        mult_one(1, 0)
-        quant_one(1, 0)
-        chain(2)
-        step_one(1, 1)
-        sigmoid_one(1, 1)
-        mx_one(0, 0)
-        mx_one(0, 1)
-        mx_one(1, 0)
-        mult_one(1, 1)
-        quant_one(1, 1)
-        squares_one(0)
-        scale_s(2)
-        chain_one(0)
-        scale_v(2)
+        squares(2, 0, True)
+        squares(2, 1, False)
+        mult(3, 1, 0, 128)
+        quant(3, 1, 0, 128)
+        chain(2, 0, 2)
+        fill(3, 2, 128, 128, [])
+        sigmoid(3, 2, 128, 128)
+        fill(3, 3, 128, 128, [])
+        sigmoid(3, 3, 128, 128)
+        mx_pass(3, 0, 0, "t", 0, 512)
+        mx_pass(3, 0, 1, "t", 0, 512)
+        mx_pass(3, 1, 0, "t", 0, 512)
+        mult(3, 1, 128, 128)
+        quant(3, 1, 128, 128)
+        squares(3, 0, True)
+        scale("s", 2, 1, rs[(2, 0)][:, 1:2])
+        chain(3, 0, 1)
+        scale("v", 2, 0, rs[(2, 0)][:, 0:1])
         store(2)
-        mx_one(1, 1)
-        squares_one(1)
-        scale_one("s", 0)
-        store_one(0)
-        chain_one(1)
-        scale_one("v", 1)
-        store_one(1)
+        mx_pass(3, 1, 1, "t", 0, 512)
+        squares(3, 1, False)
+        scale("s", 3, 0, rs[(3, 0)][:])
+        store_block(3, 0)
+        chain(3, 1, 1)
+        scale("v", 3, 1, rs[(3, 1)][:])
+        store_block(3, 1)

@@ -157,10 +157,26 @@ def tile_hybonetconv_pb_kernel(tc, q_neg, k, h, adj, att_bias, att_scale, out):
             else:
                 nc.scalar.copy(out=dst[:].bitcast(F32), in_=tr[key][:])
 
+        def copy_k(engine, key, gu):
+            dst = kT[gu][:].rearrange("p (w d x) -> p w d x", w=2, d=2)
+            src = tr[key][:].bitcast(BF16).rearrange("p (w x d) -> p w d x", w=2, d=2)
+            if engine == "v":
+                nc.vector.tensor_copy(out=dst, in_=src)
+            else:
+                nc.scalar.copy(out=dst, in_=src)
+
+        def copy_k_half(engine, key, e):
+            dst = kT[0][:].rearrange("p (w d e c) -> p w d e c", w=2, d=2, e=2)[:, :, :, e, :]
+            src = tr[key][:].bitcast(BF16).rearrange("p (w c d) -> p w d c", w=2, d=2)
+            if engine == "v":
+                nc.vector.tensor_copy(out=dst, in_=src)
+            else:
+                nc.scalar.copy(out=dst, in_=src)
+
         def fill(c, gu, lo, w, extra, dense=False):
             key = (c, gu, lo)
             acc[key] = ps_c.tile([P, 2 * w], F32, name="acc", tag="acc")
-            kv = kT[gu][:].rearrange("p (w c e) -> p w c e", w=2, e=2)
+            kv = kT[gu][:].rearrange("p (w d e c) -> p w d e c", w=2, d=2, e=2)
             qv = qT[c][:].rearrange("p (w c e) -> p w c e", w=2, e=2)
             stride = 1 if (len(extra) > 4 or dense) else 2
             n = 0
@@ -169,7 +185,7 @@ def tile_hybonetconv_pb_kernel(tc, q_neg, k, h, adj, att_bias, att_scale, out):
                     for ed in range(2):
                         nc.tensor.matmul(
                             out=acc[key][:, e * w:(e + 1) * w],
-                            lhsT=kv[:, wd, e * P:(e + 1) * P, ed],
+                            lhsT=kv[:, wd, ed, e, :],
                             rhs=qv[:, wd, lo:lo + w, ed],
                             start=(wd == 0 and ed == 0),
                             stop=(wd == 1 and ed == 1),
@@ -294,19 +310,19 @@ def tile_hybonetconv_pb_kernel(tc, q_neg, k, h, adj, att_bias, att_scale, out):
         copy_head("v", "q0a", qT[0][:].bitcast(F32)[:, 0:256].rearrange("p (a c) -> p a c", a=2))
         copy_head("s", "q0b", qT[0][:].bitcast(F32)[:, 256:512].rearrange("p (a c) -> p a c", a=2))
         t_head("k0a", "s", k_sb[0], ((0, 0), (0, 1)))
-        copy_head("v", "k0a", kT[0][:].bitcast(F32).rearrange("p (w e c) -> p w e c", w=2, e=2)[:, :, 0, :])
+        copy_k_half("v", "k0a", 0)
         dummy(WARM2, 128)
         t_head("k0b", "s", k_sb[0], ((1, 0), (1, 1)))
-        copy_head("s", "k0b", kT[0][:].bitcast(F32).rearrange("p (w e c) -> p w e c", w=2, e=2)[:, :, 1, :])
+        copy_k_half("s", "k0b", 1)
         dummy(WARM2, 128)
         for f in t_rows_list("k1", k_sb[1]):
             f()
-        copy_out("v", "k1", kT[1])
+        copy_k("v", "k1", 1)
         fill(0, 0, 0, 256, t_rows_list("k2", k_sb[2]))
-        copy_out("v", "k2", kT[2])
+        copy_k("v", "k2", 2)
         sigmoid(0, 0, 0, 256)
         fill(0, 1, 0, 256, t_rows_list("k3", k_sb[3]))
-        copy_out("v", "k3", kT[3])
+        copy_k("v", "k3", 3)
         sigmoid(0, 1, 0, 256)
         fill(0, 2, 0, 256, t_rows_list("q1", q_sb[1]) + t_adj_list(0, 0))
         copy_out("v", "q1", qT[1])

@@ -157,26 +157,10 @@ def tile_hybonetconv_pb_kernel(tc, q_neg, k, h, adj, att_bias, att_scale, out):
             else:
                 nc.scalar.copy(out=dst[:].bitcast(F32), in_=tr[key][:])
 
-        def copy_k(engine, key, gu):
-            dst = kT[gu][:].rearrange("p (w d x) -> p w d x", w=2, d=2)
-            src = tr[key][:].bitcast(BF16).rearrange("p (w x d) -> p w d x", w=2, d=2)
-            if engine == "v":
-                nc.vector.tensor_copy(out=dst, in_=src)
-            else:
-                nc.scalar.copy(out=dst, in_=src)
-
-        def copy_k_half(engine, key, e):
-            dst = kT[0][:].rearrange("p (w d e c) -> p w d e c", w=2, d=2, e=2)[:, :, :, e, :]
-            src = tr[key][:].bitcast(BF16).rearrange("p (w c d) -> p w d c", w=2, d=2)
-            if engine == "v":
-                nc.vector.tensor_copy(out=dst, in_=src)
-            else:
-                nc.scalar.copy(out=dst, in_=src)
-
         def fill(c, gu, lo, w, extra, dense=False):
             key = (c, gu, lo)
             acc[key] = ps_c.tile([P, 2 * w], F32, name="acc", tag="acc")
-            kv = kT[gu][:].rearrange("p (w d e c) -> p w d e c", w=2, d=2, e=2)
+            kv = kT[gu][:].rearrange("p (w c e) -> p w c e", w=2, e=2)
             qv = qT[c][:].rearrange("p (w c e) -> p w c e", w=2, e=2)
             stride = 1 if (len(extra) > 4 or dense) else 2
             n = 0
@@ -185,14 +169,14 @@ def tile_hybonetconv_pb_kernel(tc, q_neg, k, h, adj, att_bias, att_scale, out):
                     for ed in range(2):
                         nc.tensor.matmul(
                             out=acc[key][:, e * w:(e + 1) * w],
-                            lhsT=kv[:, wd, ed, e, :],
+                            lhsT=kv[:, wd, e * P:(e + 1) * P, ed],
                             rhs=qv[:, wd, lo:lo + w, ed],
                             start=(wd == 0 and ed == 0),
                             stop=(wd == 1 and ed == 1),
                         )
-                        if n % stride == 0 and n // stride < len(extra):
-                            extra[n // stride]()
                         n += 1
+            for f in extra:
+                f()
 
         def sigmoid(c, gu, lo, w):
             g, u = divmod(gu, 2)
@@ -310,19 +294,19 @@ def tile_hybonetconv_pb_kernel(tc, q_neg, k, h, adj, att_bias, att_scale, out):
         copy_head("v", "q0a", qT[0][:].bitcast(F32)[:, 0:256].rearrange("p (a c) -> p a c", a=2))
         copy_head("s", "q0b", qT[0][:].bitcast(F32)[:, 256:512].rearrange("p (a c) -> p a c", a=2))
         t_head("k0a", "s", k_sb[0], ((0, 0), (0, 1)))
-        copy_k_half("v", "k0a", 0)
+        copy_head("v", "k0a", kT[0][:].bitcast(F32).rearrange("p (w e c) -> p w e c", w=2, e=2)[:, :, 0, :])
         dummy(WARM2, 128)
         t_head("k0b", "s", k_sb[0], ((1, 0), (1, 1)))
-        copy_k_half("s", "k0b", 1)
+        copy_head("s", "k0b", kT[0][:].bitcast(F32).rearrange("p (w e c) -> p w e c", w=2, e=2)[:, :, 1, :])
         dummy(WARM2, 128)
         for f in t_rows_list("k1", k_sb[1]):
             f()
-        copy_k("v", "k1", 1)
+        copy_out("v", "k1", kT[1])
         fill(0, 0, 0, 256, t_rows_list("k2", k_sb[2]))
-        copy_k("v", "k2", 2)
+        copy_out("v", "k2", kT[2])
         sigmoid(0, 0, 0, 256)
         fill(0, 1, 0, 256, t_rows_list("k3", k_sb[3]))
-        copy_k("v", "k3", 3)
+        copy_out("v", "k3", kT[3])
         sigmoid(0, 1, 0, 256)
         fill(0, 2, 0, 256, t_rows_list("q1", q_sb[1]) + t_adj_list(0, 0))
         copy_out("v", "q1", qT[1])

from contextlib import ExitStack

import concourse.mybir as mybir
from concourse.masks import make_identity

BF16 = mybir.dt.bfloat16
F32 = mybir.dt.float32
U32 = mybir.dt.uint32
U8 = mybir.dt.uint8
FP8X4 = mybir.dt.float8_e4m3fn_x4
ACT = mybir.ActivationFunctionType
ALU = mybir.AluOpType

P = 128
FLOPS = 2 * 1024 * 1024 * 512 * 2
WARM = 4
WARM2 = 1
TAILD = 1
SPLIT_LAST = True


def tile_hybonetconv_pb_kernel(tc, q_neg, k, h, adj, att_bias, att_scale, out):
    nc = tc.nc
    with ExitStack() as ctx:
        keep = ctx.enter_context(tc.tile_pool(name="keep", bufs=1))
        work = ctx.enter_context(tc.tile_pool(name="work", bufs=3))
        ps_c = ctx.enter_context(tc.psum_pool(name="ps_c", bufs=3))
        ps_t = ctx.enter_context(tc.psum_pool(name="ps_t", bufs=3))
        ps_s = ctx.enter_context(tc.psum_pool(name="ps_s", bufs=2))
        ctx.enter_context(tc.manual_schedule())

        q_v = q_neg.rearrange("(c p b) d -> c p (b d)", p=P, b=2)
        k_v = k.rearrange("(c p b) d -> c p (b d)", p=P, b=2)
        k_vb = k.rearrange("(c p b) d -> c b p d", p=P, b=2)
        adj_v = adj.rearrange("(c p b) j -> c p (b j)", p=P, b=2)
        h_v = h.rearrange("(g u p e) f -> g p u (e f)", g=2, u=2, p=P, e=2)
        out_v = out.rearrange("(c p b) f -> c p (b f)", p=P, b=2)
        out_vb = out.rearrange("(c p b) f -> c b p f", p=P, b=2)

        ident = keep.tile([P, P], F32, name="ident")
        make_identity(nc, ident[:])
        bias_bf = keep.tile([P, 1], BF16, name="bias_bf")
        scale_bf = keep.tile([P, 1], BF16, name="scale_bf")
        nc.scalar.dma_start(out=scale_bf[:], in_=att_scale.partition_broadcast(P))
        nc.scalar.dma_start(out=bias_bf[:], in_=att_bias.partition_broadcast(P))
        neghalf = keep.tile([P, 2], F32, name="neghalf")
        zeros = keep.tile([P, 256], F32, name="zeros")
        nc.vector.memset(zeros[:], 0.0)
        nc.vector.memset(neghalf[:], -0.5)
        warm_in = keep.tile([P, 1], F32, name="warm_in")
        warm_out = keep.tile([P, 1], F32, name="warm_out")
        nc.vector.memset(warm_in[:], 0.0)
        nc.scalar.activation(out=warm_out[:], in_=warm_in[:], func=ACT.Sigmoid)

        q_sb = [keep.tile([P, 1024], BF16, name="q_sb%d" % c) for c in range(4)]
        k_sb = [keep.tile([P, 1024], BF16, name="k_sb%d" % c) for c in range(4)]
        adj_sb = [keep.tile([P, 2048], BF16, name="adj_sb%d" % c) for c in range(4)]
        h_sb = [keep.tile([P, 2048], BF16, name="h_sb%d" % g) for g in range(2)]

        def load(kind, c):
            if kind == "q":
                nc.sync.dma_start(out=q_sb[c][:], in_=q_v[c])
            elif kind == "k":
                nc.sync.dma_start(out=k_sb[c][:], in_=k_v[c])
            elif kind == "k0":
                nc.sync.dma_start(out=k_sb[0][:, c * 512:(c + 1) * 512], in_=k_vb[0][c])
            elif kind == "a":
                nc.sync.dma_start(out=adj_sb[c][:], in_=adj_v[c])
            else:
                nc.sync.dma_start(out=h_sb[c][:].rearrange("p (u x) -> p u x", u=2), in_=h_v[c])

        for kind, c in (("q", 0), ("k0", 0), ("k0", 1), ("k", 1), ("k", 2), ("k", 3), ("q", 1), ("a", 0), ("h", 0), ("h", 1), ("a", 1), ("q", 2), ("a", 2), ("q", 3), ("a", 3)):
            load(kind, c)

        arg_mul = keep.tile([P, 1], F32, name="arg_mul")
        arg_add = keep.tile([P, 1], F32, name="arg_add")
        rec = keep.tile([P, 1], F32, name="rec")
        nc.vector.reciprocal(out=rec[:], in_=scale_bf[:])
        nc.vector.tensor_scalar(out=arg_mul[:], in0=rec[:], scalar1=2.0, scalar2=None, op0=ALU.mult)
        nc.vector.tensor_tensor(out=arg_add[:], in0=arg_mul[:], in1=bias_bf[:], op=ALU.add)

        qT = [keep.tile([P, 1024], BF16, name="qT%d" % c) for c in range(4)]
        kT = [keep.tile([P, 1024], BF16, name="kT%d" % c) for c in range(4)]
        hg = [keep.tile([P, 2048], BF16, name="hg%d" % g, align_bytes=64) for g in range(2)]
        h_codes = [keep.tile([P, 512], U32, name="h_codes%d" % g, align_bytes=64) for g in range(2)]
        h_scales = [keep.tile([P, 512], U8, name="h_scales%d" % g, align_bytes=64) for g in range(2)]
        o_sb = [keep.tile([P, 1024], F32, name="o_sb%d" % c) for c in range(4)]

        tr = {}
        acc = {}
        sig = {}
        att = {}
        codes = {}
        planes = {}
        widths = {}
        sup = {}
        stat = {}
        rs = {}

        def dummy(n, width):
            for i in range(n):
                scratch = ps_c.tile([P, width], F32, name="acc", tag="acc")
                nc.tensor.matmul(out=scratch[:], lhsT=zeros[:, 0:P], rhs=zeros[:, 0:width], start=True, stop=True)

        def new_tr(key):
            tr[key] = ps_t.tile([P, 512], F32, name="tr", tag="tr")

        def t_rows(key, src, n):
            wd, b = divmod(n, 2)
            if n == 0:
                new_tr(key)
            nc.tensor.transpose(
                tr[key][:, n * P:(n + 1) * P],
                src[:].bitcast(F32)[:, b * 256 + wd * P: b * 256 + (wd + 1) * P],
                ident[:],
            )

        def t_rows_list(key, src):
            return [(lambda n=n: t_rows(key, src, n)) for n in range(4)]

        def t_head(key, pool, src, pieces):
            if pool == "s":
                tr[key] = ps_s.tile([P, 256], F32, name="sup", tag="sup")
            else:
                tr[key] = ps_t.tile([P, 256], F32, name="tr", tag="tr")
            for n, (b, wd) in enumerate(pieces):
                nc.tensor.transpose(
                    tr[key][:, n * P:(n + 1) * P],
                    src[:].bitcast(F32)[:, b * 256 + wd * P: b * 256 + (wd + 1) * P],
                    ident[:],
                )

        def copy_head(engine, key, dst):
            src = tr[key][:].rearrange("p (a c) -> p a c", a=2)
            if engine == "v":
                nc.vector.tensor_copy(out=dst, in_=src)
            else:
                nc.scalar.copy(out=dst, in_=src)

        def t_adj(c, g, n):
            u, b = divmod(n, 2)
            if n == 0:
                new_tr(("a", c, g))
            gu = 2 * g + u
            nc.tensor.transpose(
                tr[("a", c, g)][:, n * P:(n + 1) * P],
                adj_sb[c][:].bitcast(F32)[:, b * 512 + gu * P: b * 512 + (gu + 1) * P],
                ident[:],
            )

        def t_adj_list(c, g):
            return [(lambda n=n: t_adj(c, g, n)) for n in range(4)]

        def copy_out(engine, key, dst):
            if engine == "v":
                nc.vector.tensor_copy(out=dst[:].bitcast(F32), in_=tr[key][:])
            else:
                nc.scalar.copy(out=dst[:].bitcast(F32), in_=tr[key][:])

        def fill(c, gu, lo, w, extra, dense=False):
            key = (c, gu, lo)
            acc[key] = ps_c.tile([P, 2 * w], F32, name="acc", tag="acc")
            kv = kT[gu][:].rearrange("p (w c e) -> p w c e", w=2, e=2)
            qv = qT[c][:].rearrange("p (w c e) -> p w c e", w=2, e=2)
            stride = 1 if (len(extra) > 4 or dense) else 2
            n = 0
            for e in range(2):
                for wd in range(2):
                    for ed in range(2):
                        nc.tensor.matmul(
                            out=acc[key][:, e * w:(e + 1) * w],
                            lhsT=kv[:, wd, e * P:(e + 1) * P, ed],
                            rhs=qv[:, wd, lo:lo + w, ed],
                            start=(wd == 0 and ed == 0),
                            stop=(wd == 1 and ed == 1),
                        )
                        n += 1
            for f in extra:
                f()

        def sigmoid(c, gu, lo, w):
            g, u = divmod(gu, 2)
            if u == 0:
                sig[(c, g, lo)] = work.tile([P, 4 * w], F32, name="sig", tag="sig", bufs=4)
            nc.scalar.activation(
                out=sig[(c, g, lo)][:, u * 2 * w:(u + 1) * 2 * w].rearrange("p (c e) -> p c e", e=2),
                in_=acc[(c, gu, lo)][:].rearrange("p (e c) -> p c e", e=2),
                func=ACT.Sigmoid,
                bias=arg_add[:],
                scale=arg_mul[:],
            )

        def mult(c, g, lo, w):
            att[(c, g, lo)] = work.tile([P, 4 * w], BF16, name="att", tag="att", align_bytes=64)
            nc.vector.tensor_tensor(
                out=att[(c, g, lo)][:].rearrange("p (c u e) -> p c u e", u=2, e=2),
                in0=sig[(c, g, lo)][:].rearrange("p (u c e) -> p c u e", u=2, e=2),
                in1=tr[("a", c, g)][:].bitcast(BF16).rearrange(
                    "p (u c e) -> p c u e", u=2, e=2)[:, lo:lo + w, :, :],
                op=ALU.mult,
            )

        def quant(c, g, lo, w):
            widths[(c, g, lo)] = w
            codes[(c, g, lo)] = keep.tile([P, w], U32, name="codes_%d_%d_%d" % (c, g, lo), align_bytes=64)
            planes[(c, g, lo)] = keep.tile([P, w], U8, name="planes_%d_%d_%d" % (c, g, lo), align_bytes=64)
            nc.vector.quantize_mx(
                out=codes[(c, g, lo)][:].bitcast(FP8X4), scales=planes[(c, g, lo)][:], in_=att[(c, g, lo)][:]
            )

        def regroup_h(engine, g, lo, w):
            dst = hg[g][:, 4 * lo:4 * (lo + w)].rearrange("p (c i t) -> p c t i", i=4, t=4)
            src = h_sb[g][:].rearrange("p (t f) -> p t f", t=4)[:, :, lo:lo + w].rearrange(
                "p t (c i) -> p c t i", i=4)
            if engine == "v":
                nc.vector.tensor_copy(out=dst, in_=src)
            else:
                nc.scalar.copy(out=dst, in_=src)

        def quant_h(g):
            nc.vector.quantize_mx(
                out=h_codes[g][:].bitcast(FP8X4), scales=h_scales[g][:], in_=hg[g][:]
            )

        def mx_pass(c, b, g, pool, flo, fw):
            key = (c, b, flo)
            if g == 0:
                if pool == "s":
                    sup[key] = ps_s.tile([P, fw], F32, name="sup", tag="sup")
                elif pool == "t":
                    sup[key] = ps_t.tile([P, fw], F32, name="tr", tag="tr")
                else:
                    sup[key] = ps_c.tile([P, fw], F32, name="acc", tag="acc")
            if widths.get((c, g, 0), 0) == 256:
                cd, pl = codes[(c, g, 0)][:, b * P:(b + 1) * P], planes[(c, g, 0)][:, b * P:(b + 1) * P]
            else:
                cd, pl = codes[(c, g, b * P)][:], planes[(c, g, b * P)][:]
            nc.tensor.matmul_mx(
                out=sup[key][:],
                lhsT=cd.bitcast(FP8X4),
                lhsT_scale=pl,
                rhs=h_codes[g][:, flo:flo + fw].bitcast(FP8X4),
                rhs_scale=h_scales[g][:, flo:flo + fw],
                start=(g == 0),
                stop=(g == 1),
            )

        def squares(c, b, first):
            if first:
                stat[c] = work.tile([P, 4], F32, name="stat", tag="stat", bufs=4)
            junk = work.tile([P, 512], BF16, name="junk", tag="junk", bufs=2)
            nc.scalar.activation(
                out=junk[:, 0:511], in_=sup[(c, b, 0)][:, 1:512], func=ACT.Square,
                accum_out=stat[c][:, b:b + 1],
            )
            nc.scalar.activation(
                out=stat[c][:, 2 + b:3 + b], in_=sup[(c, b, 0)][:, 0:1], func=ACT.Square
            )

        def chain(c, b, n):
            nl = work.tile([P, n], F32, name="nl", tag="nl")
            al = work.tile([P, n], F32, name="al", tag="al")
            cl = work.tile([P, n], F32, name="cl", tag="cl")
            rs[(c, b)] = work.tile([P, n], F32, name="rs", tag="rs", bufs=4)
            nc.vector.tensor_tensor(
                out=nl[:], in0=stat[c][:, b:b + n], in1=stat[c][:, 2 + b:2 + b + n], op=ALU.subtract)
            nc.vector.scalar_tensor_tensor(
                out=al[:], in0=nl[:], scalar=-1.0, in1=nl[:], op0=ALU.mult, op1=ALU.max
            )
            nc.vector.tensor_scalar(out=cl[:], in0=al[:], scalar1=1e-6, scalar2=None, op0=ALU.max)
            nc.gpsimd.tensor_tensor(out=rs[(c, b)][:], in0=cl[:], in1=neghalf[:, 0:n], op=ALU.pow)

        def scale(engine, c, b, r, flo=0, fw=512):
            dst = o_sb[c][:, b * 512 + flo:b * 512 + flo + fw]
            if engine == "v":
                nc.vector.tensor_scalar(out=dst, in0=sup[(c, b, flo)][:], scalar1=r, scalar2=None, op0=ALU.mult)
            else:
                nc.scalar.activation(out=dst, in_=sup[(c, b, flo)][:], func=ACT.Copy, scale=r)

        def store(c):
            nc.sync.dma_start(out=out_v[c], in_=o_sb[c][:])

        def store_block(c, b):
            nc.sync.dma_start(out=out_vb[c][b], in_=o_sb[c][:, b * 512:(b + 1) * 512])

        def mx_all(c):
            for b in range(2):
                for g in range(2):
                    mx_pass(c, b, g, "s", 0, 512)

        dummy(WARM, 256)
        t_head("q0a", "t", q_sb[0], ((0, 0), (1, 0)))
        t_head("q0b", "t", q_sb[0], ((0, 1), (1, 1)))
        copy_head("v", "q0a", qT[0][:].bitcast(F32)[:, 0:256].rearrange("p (a c) -> p a c", a=2))
        copy_head("s", "q0b", qT[0][:].bitcast(F32)[:, 256:512].rearrange("p (a c) -> p a c", a=2))
        t_head("k0a", "s", k_sb[0], ((0, 0), (0, 1)))
        copy_head("v", "k0a", kT[0][:].bitcast(F32).rearrange("p (w e c) -> p w e c", w=2, e=2)[:, :, 0, :])
        dummy(WARM2, 128)
        t_head("k0b", "s", k_sb[0], ((1, 0), (1, 1)))
        copy_head("s", "k0b", kT[0][:].bitcast(F32).rearrange("p (w e c) -> p w e c", w=2, e=2)[:, :, 1, :])
        dummy(WARM2, 128)
        for f in t_rows_list("k1", k_sb[1]):
            f()
        copy_out("v", "k1", kT[1])
        fill(0, 0, 0, 256, t_rows_list("k2", k_sb[2]))
        copy_out("v", "k2", kT[2])
        sigmoid(0, 0, 0, 256)
        fill(0, 1, 0, 256, t_rows_list("k3", k_sb[3]))
        copy_out("v", "k3", kT[3])
        sigmoid(0, 1, 0, 256)
        fill(0, 2, 0, 256, t_rows_list("q1", q_sb[1]) + t_adj_list(0, 0))
        copy_out("v", "q1", qT[1])
        sigmoid(0, 2, 0, 256)
        mult(0, 0, 0, 256)
        fill(0, 3, 0, 256, t_adj_list(0, 1))
        sigmoid(0, 3, 0, 256)
        regroup_h("s", 0, 0, 256)
        regroup_h("v", 1, 0, 512)
        quant(0, 0, 0, 256)
        mult(0, 1, 0, 256)
        fill(1, 0, 0, 256, [])
        sigmoid(1, 0, 0, 256)
        regroup_h("s", 0, 256, 256)
        quant(0, 1, 0, 256)
        quant_h(1)
        fill(1, 1, 0, 256, t_adj_list(1, 0))
        sigmoid(1, 1, 0, 256)
        quant_h(0)
        mult(1, 0, 0, 256)
        fill(1, 2, 0, 256, t_rows_list("q2", q_sb[2]) + t_adj_list(1, 1))
        copy_out("v", "q2", qT[2])
        sigmoid(1, 2, 0, 256)
        quant(1, 0, 0, 256)
        fill(1, 3, 0, 256, [])
        sigmoid(1, 3, 0, 256)
        mult(1, 1, 0, 256)
        mx_all(0)
        squares(0, 0, True)
        squares(0, 1, False)
        quant(1, 1, 0, 256)
        fill(2, 0, 0, 256, t_adj_list(2, 0))
        sigmoid(2, 0, 0, 256)
        chain(0, 0, 2)
        scale("v", 0, 0, rs[(0, 0)][:, 0:1])
        scale("s", 0, 1, rs[(0, 0)][:, 1:2])
        store(0)
        fill(2, 1, 0, 256, t_rows_list("q3", q_sb[3]))
        sigmoid(2, 1, 0, 256)
        mult(2, 0, 0, 256)
        copy_out("v", "q3", qT[3])
        quant(2, 0, 0, 256)
        fill(2, 2, 0, 256, t_adj_list(2, 1))
        sigmoid(2, 2, 0, 256)
        mx_all(1)
        squares(1, 0, True)
        squares(1, 1, False)
        chain(1, 0, 2)
        fill(2, 3, 0, 256, t_adj_list(3, 0))
        sigmoid(2, 3, 0, 256)
        scale("s", 1, 1, rs[(1, 0)][:, 1:2])
        mult(2, 1, 0, 256)
        scale("v", 1, 0, rs[(1, 0)][:, 0:1])
        quant(2, 1, 0, 256)
        store(1)
        fill(3, 0, 0, 256, t_adj_list(3, 1))
        sigmoid(3, 0, 0, 256)
        fill(3, 1, 0, 256, [])
        sigmoid(3, 1, 0, 256)
        mult(3, 0, 0, 256)
        quant(3, 0, 0, 256)
        fill(3, 2, 0, 128, [])
        sigmoid(3, 2, 0, 128)
        fill(3, 3, 0, 128, [])
        sigmoid(3, 3, 0, 128)
        mx_all(2)
        squares(2, 0, True)
        squares(2, 1, False)
        mult(3, 1, 0, 128)
        quant(3, 1, 0, 128)
        chain(2, 0, 2)
        fill(3, 2, 128, 128, [])
        sigmoid(3, 2, 128, 128)
        fill(3, 3, 128, 128, [])
        sigmoid(3, 3, 128, 128)
        mx_pass(3, 0, 0, "t", 0, 512)
        mx_pass(3, 0, 1, "t", 0, 512)
        mx_pass(3, 1, 0, "t", 0, 512)
        mult(3, 1, 128, 128)
        quant(3, 1, 128, 128)
        squares(3, 0, True)
        scale("s", 2, 1, rs[(2, 0)][:, 1:2])
        chain(3, 0, 1)
        scale("v", 2, 0, rs[(2, 0)][:, 0:1])
        store(2)
        mx_pass(3, 1, 1, "t", 0, 512)
        squares(3, 1, False)
        scale("s", 3, 0, rs[(3, 0)][:])
        store_block(3, 0)
        chain(3, 1, 1)
        scale("v", 3, 1, rs[(3, 1)][:])
        store_block(3, 1)
